import numpy as np
import ml_dtypes


def mxq(x, axis, fmt="e4m3"):
    dtype, down = {"e4m3": (ml_dtypes.float8_e4m3fn, 7), "e5m2": (ml_dtypes.float8_e5m2, 14)}[fmt]
    v = np.moveaxis(np.asarray(x, np.float32).astype(ml_dtypes.bfloat16).astype(np.float64), axis, -1)
    blocks = v.reshape(v.shape[:-1] + (-1, 32))
    amax = np.abs(blocks).max(-1, keepdims=True)
    byte = np.maximum(np.where(amax > 0, np.frexp(amax)[1] - 1 + 127, 0) - down, 1)
    scale = np.exp2(byte - 127.0)
    codes = (blocks / scale).astype(np.float32).astype(dtype).astype(np.float64)
    return np.moveaxis((codes * scale).reshape(v.shape), -1, axis)


WIDE = False


def mx_kscale(k):
    if not WIDE:
        return np.ones(k)
    levels = np.array([10, -10, 5, -5, 0])
    if k % 512:
        return np.exp2(np.random.permutation(np.resize(levels, k // 32))).repeat(32)
    a = np.empty((k // 512, 16))
    for p in range(k // 512):
        a[p, :8] = np.random.permutation(np.resize(levels, 8))
        for g in range(8):
            far = levels[np.abs(levels - a[p, g]) >= 10]
            a[p, g + 8] = far[np.random.randint(len(far))]
    return np.exp2(a.ravel()).repeat(32)


BF16 = ml_dtypes.bfloat16


def bf(x):
    return np.asarray(x, np.float32).astype(BF16)


def f64(x):
    return np.asarray(x).astype(np.float64)


B, L, S, D, DA, H, MLP = 4, 3, 2048, 256, 512, 16, 4096
EPS = 1e-5


def layer_norm(u, g, b):
    mu = u.mean(-1, keepdims=True)
    var = ((u - mu) ** 2).mean(-1, keepdims=True)
    return (u - mu) / np.sqrt(var + EPS) * g + b


def setup_inputs():
    s = mx_kscale(DA)
    r = np.random.standard_normal
    return {"h_attn": bf(r((B, S, DA)) * 2.0 * s), "x": bf(r((B, S, D))),
            "attn_out_W": bf(r((DA, D)) * 0.5 / np.sqrt(DA) / s[:, None]), "attn_out_b": bf(r(D) * 0.2),
            "attn_norm_g": bf(1.0 + 0.1 * r(D)), "attn_norm_b": bf(r(D) * 0.1)}


def reference(h_attn, x, attn_out_W, attn_out_b, attn_norm_g, attn_norm_b):
    o = (mxq(f64(h_attn), 2, "e4m3") @ mxq(f64(attn_out_W), 0, "e4m3")) + f64(attn_out_b)
    return f64(x) + layer_norm(o, f64(attn_norm_g), f64(attn_norm_b))

@@ -1,0 +1,299 @@
+from contextlib import ExitStack
+
+import concourse.mybir as mybir
+from concourse.masks import make_identity
+
+F32 = mybir.dt.float32
+BF16 = mybir.dt.bfloat16
+U32 = mybir.dt.uint32
+U8 = mybir.dt.uint8
+FP8X4 = mybir.dt.float8_e4m3fn_x4
+ALU = mybir.AluOpType
+ACT = mybir.ActivationFunctionType
+
+P = 128
+PACK = 4
+ROWS = 4 * 2048
+K = 512
+FEAT = 256
+HALVES = FEAT // P
+WORDS = K // 2
+TILES = ROWS // P
+PAIR = 2
+PAIRS = TILES // PAIR
+CHUNK = 4
+EPS = 1e-5
+VECTOR_SHARE = 5
+
+FLOPS = 2 * ROWS * K * FEAT
+
+
+def tile_dcadecoderblock_pb_t_kernel(
+    tc, h_attn, x, attn_out_W, attn_out_b, attn_norm_g, attn_norm_b, out
+):
+    nc = tc.nc
+    h_rows = h_attn.flatten_outer_dims().rearrange("(p j) k -> p j k", j=TILES)
+    x_rows = x.flatten_outer_dims().rearrange("(p j) n -> p j n", j=TILES)
+    out_rows = out.flatten_outer_dims().rearrange("(p j) n -> p j n", j=TILES)
+
+    with ExitStack() as stack:
+        consts = stack.enter_context(tc.tile_pool(name="consts", bufs=1))
+        loads = stack.enter_context(tc.tile_pool(name="loads", bufs=TILES // CHUNK))
+        work = stack.enter_context(tc.tile_pool(name="work", bufs=3))
+        long_lived = stack.enter_context(tc.tile_pool(name="long_lived", bufs=6))
+        results = stack.enter_context(tc.tile_pool(name="results", bufs=8))
+        psum = stack.enter_context(tc.psum_pool(name="psum", bufs=2))
+        stack.enter_context(tc.manual_schedule())
+
+        ident = consts.tile([P, P], F32)
+        make_identity(nc, ident[:])
+
+        w_raw = consts.tile([P, PACK, FEAT], BF16)
+        nc.scalar.dma_start(
+            out=w_raw[:], in_=attn_out_W.rearrange("(p t) n -> p t n", t=PACK)
+        )
+        bias_row = consts.tile([P, FEAT], BF16)
+        nc.vector.memset(bias_row[:], 0.0)
+        nc.scalar.dma_start(out=bias_row[0:1, :], in_=attn_out_b.rearrange("(o n) -> o n", o=1))
+        norm_rows = consts.tile([P, P], BF16)
+        nc.vector.memset(norm_rows[:], 0.0)
+        nc.scalar.dma_start(
+            out=norm_rows[0:HALVES, :], in_=attn_norm_g.rearrange("(j p) -> j p", p=P)
+        )
+        nc.scalar.dma_start(
+            out=norm_rows[HALVES : 2 * HALVES, :], in_=attn_norm_b.rearrange("(j p) -> j p", p=P)
+        )
+        ones = consts.tile([P, P], BF16)
+        nc.vector.memset(ones[:], 1.0)
+        eps = consts.tile([P, 1], F32)
+        nc.vector.memset(eps[:], EPS)
+        table_warm = consts.tile([P, 1], F32)
+        nc.scalar.activation(out=table_warm[:], in_=eps[:], func=ACT.Abs_reciprocal_sqrt)
+
+        h_chunks = []
+        x_chunks = []
+        for c in range(TILES // CHUNK):
+            tiles = slice(c * CHUNK, (c + 1) * CHUNK)
+            h_sb = loads.tile([P, CHUNK * K], BF16)
+            nc.sync.dma_start(
+                out=h_sb[:].rearrange("p (i k) -> p i k", i=CHUNK), in_=h_rows[:, tiles, :]
+            )
+            h_chunks.append(h_sb)
+            x_sb = loads.tile([P, CHUNK * FEAT], BF16)
+            nc.sync.dma_start(
+                out=x_sb[:].rearrange("p (i n) -> p i n", i=CHUNK), in_=x_rows[:, tiles, :]
+            )
+            x_chunks.append(x_sb)
+
+        w_grouped = consts.tile([P, FEAT, PACK], BF16, align_bytes=64)
+        nc.vector.tensor_copy(out=w_grouped[:], in_=w_raw[:].rearrange("p t n -> p n t"))
+        w_codes = consts.tile([P, FEAT], U32, align_bytes=64)
+        w_scales = consts.tile([P, FEAT], U8, align_bytes=64)
+        nc.vector.quantize_mx(
+            out=w_codes[:].bitcast(FP8X4),
+            scales=w_scales[:],
+            in_=w_grouped[:].rearrange("p n t -> p (n t)"),
+        )
+        norm_rows_f32 = consts.tile([P, P], F32)
+        nc.vector.tensor_copy(out=norm_rows_f32[:], in_=norm_rows[:])
+        bias_all = consts.tile([P, FEAT], F32)
+        norm_cols = consts.tile([P, 2 * HALVES], F32)
+
+        def spread_constants():
+            bias_ps = psum.tile([P, FEAT], F32, tag="a_ps")
+            nc.tensor.matmul(out=bias_ps[:], lhsT=ones[:], rhs=bias_row[:], start=True, stop=True)
+            nc.vector.tensor_copy(out=bias_all[:], in_=bias_ps[:])
+            norm_ps = psum.tile([P, P], F32, tag="tT_ps")
+            nc.tensor.transpose(norm_ps[:], norm_rows_f32[:], ident[:])
+            nc.vector.tensor_copy(out=norm_cols[:], in_=norm_ps[:, 0 : 2 * HALVES])
+
+        kept = {}
+
+        def transpose_h(u):
+            first = (u * PAIR % CHUNK) * WORDS
+            h_words = h_chunks[u * PAIR // CHUNK][:].bitcast(F32)
+            hT_ps = psum.tile([P, PAIR * WORDS], F32)
+            for i in range(PAIR):
+                row = first + i * WORDS
+                for v in range(2):
+                    c = 2 * i + v
+                    nc.tensor.transpose(
+                        hT_ps[:, c * P : (c + 1) * P],
+                        h_words[:, row + v : row + WORDS : 2],
+                        ident[:],
+                    )
+            kept["hT", u] = hT_ps
+
+        def regroup_h(u):
+            grouped = work.tile([P, PAIR * P * PACK], BF16, align_bytes=64)
+            side_by_side = grouped[:].bitcast(F32).rearrange("p (i r v) -> p i r v", i=PAIR, v=2)
+            bank = kept["hT", u][:].rearrange("p (i v r) -> p i r v", i=PAIR, v=2)
+            if u % VECTOR_SHARE == VECTOR_SHARE - 1:
+                nc.vector.tensor_copy(out=side_by_side, in_=bank)
+            else:
+                nc.scalar.copy(out=side_by_side, in_=bank)
+            kept["grouped", u] = grouped
+
+        def quantise_h(u):
+            h_codes = work.tile([P, PAIR * P], U32, align_bytes=64)
+            h_scales = work.tile([P, PAIR * P], U8, align_bytes=64)
+            nc.vector.quantize_mx(
+                out=h_codes[:].bitcast(FP8X4), scales=h_scales[:], in_=kept["grouped", u][:]
+            )
+            kept["codes", u] = h_codes
+            kept["scales", u] = h_scales
+
+        def project(u):
+            a_ps = psum.tile([P, PAIR, FEAT], F32)
+            for i in range(PAIR):
+                nc.tensor.matmul_mx(
+                    out=a_ps[:, i, :],
+                    lhsT=kept["codes", u][:, i * P : (i + 1) * P].bitcast(FP8X4),
+                    lhsT_scale=kept["scales", u][:, i * P : (i + 1) * P],
+                    rhs=w_codes[:].bitcast(FP8X4),
+                    rhs_scale=w_scales[:],
+                    start=True,
+                    stop=True,
+                )
+            kept["a", u] = a_ps
+
+        def add_bias(u):
+            o = long_lived.tile([P, PAIR, FEAT], F32)
+            row_sum = work.tile([P, PAIR], F32)
+            for i in range(PAIR):
+                nc.vector.scalar_tensor_tensor(
+                    out=o[:, i, :],
+                    in0=kept["a", u][:, i, :],
+                    scalar=1.0,
+                    in1=bias_all[:],
+                    op0=ALU.mult,
+                    op1=ALU.add,
+                    accum_out=row_sum[:, i : i + 1],
+                )
+            kept["o", u] = o
+            kept["row_sum", u] = row_sum
+
+        def negate_mean(u):
+            neg_mean = long_lived.tile([P, PAIR], F32)
+            nc.gpsimd.tensor_scalar(
+                out=neg_mean[:],
+                in0=kept["row_sum", u][:],
+                scalar1=-1.0 / FEAT,
+                scalar2=0.0,
+                op0=ALU.mult,
+                op1=ALU.add,
+            )
+            kept["neg_mean", u] = neg_mean
+
+        def sum_squares(u):
+            squares = work.tile([P, PAIR, FEAT], F32)
+            sum_sq = work.tile([P, PAIR], F32)
+            for i in range(PAIR):
+                nc.scalar.activation(
+                    out=squares[:, i, :],
+                    in_=kept["o", u][:, i, :],
+                    func=ACT.Square,
+                    bias=kept["neg_mean", u][:, i : i + 1],
+                    accum_out=sum_sq[:, i : i + 1],
+                )
+            kept["sum_sq", u] = sum_sq
+
+        def inverse_root(u):
+            rstd = work.tile([P, PAIR], F32)
+            nc.scalar.activation(
+                out=rstd[:],
+                in_=kept["sum_sq", u][:],
+                func=ACT.Abs_reciprocal_sqrt,
+                scale=1.0 / FEAT,
+                bias=eps[:],
+            )
+            kept["rstd", u] = rstd
+
+        def normalise(u):
+            t = work.tile([P, PAIR, FEAT], F32)
+            for i in range(PAIR):
+                nc.gpsimd.tensor_scalar(
+                    out=t[:, i, :],
+                    in0=kept["o", u][:, i, :],
+                    scalar1=kept["neg_mean", u][:, i : i + 1],
+                    scalar2=kept["rstd", u][:, i : i + 1],
+                    op0=ALU.add,
+                    op1=ALU.mult,
+                )
+            kept["t", u] = t
+
+        def features_to_partitions(u):
+            tT_ps = psum.tile([P, HALVES, PAIR * P], F32)
+            for j in range(HALVES):
+                for i in range(PAIR):
+                    nc.tensor.transpose(
+                        tT_ps[:, j, i * P : (i + 1) * P],
+                        kept["t", u][:, i, j * P : (j + 1) * P],
+                        ident[:],
+                    )
+            kept["tT", u] = tT_ps
+
+        def gain_and_shift(u):
+            yT = work.tile([P, HALVES, PAIR * P], F32)
+            for j in range(HALVES):
+                nc.scalar.activation(
+                    out=yT[:, j, :],
+                    in_=kept["tT", u][:, j, :],
+                    func=ACT.Identity,
+                    scale=norm_cols[:, j : j + 1],
+                    bias=norm_cols[:, HALVES + j : HALVES + j + 1],
+                )
+            kept["yT", u] = yT
+
+        def rows_to_partitions(u):
+            y_ps = psum.tile([P, PAIR, FEAT], F32)
+            for i in range(PAIR):
+                for j in range(HALVES):
+                    nc.tensor.transpose(
+                        y_ps[:, i, j * P : (j + 1) * P],
+                        kept["yT", u][:, j, i * P : (i + 1) * P],
+                        ident[:],
+                    )
+            kept["y", u] = y_ps
+
+        def add_residual_and_store(u):
+            first = (u * PAIR % CHUNK) * FEAT
+            result = results.tile([P, PAIR * FEAT], F32)
+            nc.vector.tensor_tensor(
+                out=result[:],
+                in0=kept["y", u][:].rearrange("p i n -> p (i n)"),
+                in1=x_chunks[u * PAIR // CHUNK][:, first : first + PAIR * FEAT],
+                op=ALU.add,
+            )
+            nc.sync.dma_start(
+                out=out_rows[:, u * PAIR : (u + 1) * PAIR, :],
+                in_=result[:].rearrange("p (i n) -> p i n", i=PAIR),
+            )
+
+        stages = [
+            transpose_h,
+            regroup_h,
+            quantise_h,
+            project,
+            add_bias,
+            negate_mean,
+            sum_squares,
+            inverse_root,
+            normalise,
+            features_to_partitions,
+            gain_and_shift,
+            rows_to_partitions,
+            add_residual_and_store,
+        ]
+
+        def one_round(s):
+            for n, stage in reversed(list(enumerate(stages))):
+                if 0 <= s - n < PAIRS:
+                    stage(s - n)
+
+        first_product = stages.index(project)
+        for s in range(first_product):
+            one_round(s)
+        spread_constants()
+        for s in range(first_product, PAIRS + len(stages) - 1):
+            one_round(s)

@@ -22,8 +22,8 @@ TILES = ROWS // P
 PAIR = 2
 PAIRS = TILES // PAIR
 CHUNK = 4
+X_LAG = 2
 EPS = 1e-5
-VECTOR_SHARE = 5
 
 FLOPS = 2 * ROWS * K * FEAT
 
@@ -41,7 +41,7 @@ def tile_dcadecoderblock_pb_t_kernel(
         loads = stack.enter_context(tc.tile_pool(name="loads", bufs=TILES // CHUNK))
         work = stack.enter_context(tc.tile_pool(name="work", bufs=3))
         long_lived = stack.enter_context(tc.tile_pool(name="long_lived", bufs=6))
-        results = stack.enter_context(tc.tile_pool(name="results", bufs=8))
+        results = stack.enter_context(tc.tile_pool(name="results", bufs=10))
         psum = stack.enter_context(tc.psum_pool(name="psum", bufs=2))
         stack.enter_context(tc.manual_schedule())
 
@@ -49,9 +49,7 @@ def tile_dcadecoderblock_pb_t_kernel(
         make_identity(nc, ident[:])
 
         w_raw = consts.tile([P, PACK, FEAT], BF16)
-        nc.scalar.dma_start(
-            out=w_raw[:], in_=attn_out_W.rearrange("(p t) n -> p t n", t=PACK)
-        )
+        nc.scalar.dma_start(out=w_raw[:], in_=attn_out_W.rearrange("(p t) n -> p t n", t=PACK))
         bias_row = consts.tile([P, FEAT], BF16)
         nc.vector.memset(bias_row[:], 0.0)
         nc.scalar.dma_start(out=bias_row[0:1, :], in_=attn_out_b.rearrange("(o n) -> o n", o=1))
@@ -72,18 +70,32 @@ def tile_dcadecoderblock_pb_t_kernel(
 
         h_chunks = []
         x_chunks = []
-        for c in range(TILES // CHUNK):
-            tiles = slice(c * CHUNK, (c + 1) * CHUNK)
+
+        def load_h(c, parts):
             h_sb = loads.tile([P, CHUNK * K], BF16)
-            nc.sync.dma_start(
-                out=h_sb[:].rearrange("p (i k) -> p i k", i=CHUNK), in_=h_rows[:, tiles, :]
-            )
+            step = CHUNK // parts
+            for j in range(parts):
+                nc.sync.dma_start(
+                    out=h_sb[:, j * step * K : (j + 1) * step * K].rearrange(
+                        "p (i k) -> p i k", i=step
+                    ),
+                    in_=h_rows[:, c * CHUNK + j * step : c * CHUNK + (j + 1) * step, :],
+                )
             h_chunks.append(h_sb)
+
+        def load_x(c):
             x_sb = loads.tile([P, CHUNK * FEAT], BF16)
             nc.sync.dma_start(
-                out=x_sb[:].rearrange("p (i n) -> p i n", i=CHUNK), in_=x_rows[:, tiles, :]
+                out=x_sb[:].rearrange("p (i n) -> p i n", i=CHUNK),
+                in_=x_rows[:, c * CHUNK : (c + 1) * CHUNK, :],
             )
             x_chunks.append(x_sb)
+
+        for c in range(TILES // CHUNK + X_LAG):
+            if c < TILES // CHUNK:
+                load_h(c, 2 if c == 0 else 1)
+            if c >= X_LAG:
+                load_x(c - X_LAG)
 
         w_grouped = consts.tile([P, FEAT, PACK], BF16, align_bytes=64)
         nc.vector.tensor_copy(out=w_grouped[:], in_=w_raw[:].rearrange("p t n -> p n t"))
@@ -97,15 +109,19 @@ def tile_dcadecoderblock_pb_t_kernel(
         norm_rows_f32 = consts.tile([P, P], F32)
         nc.vector.tensor_copy(out=norm_rows_f32[:], in_=norm_rows[:])
         bias_all = consts.tile([P, FEAT], F32)
-        norm_cols = consts.tile([P, 2 * HALVES], F32)
+        gain_cols = consts.tile([P, HALVES], F32)
+        shift_cols = consts.tile([P, HALVES], F32)
 
         def spread_constants():
             bias_ps = psum.tile([P, FEAT], F32, tag="a_ps")
             nc.tensor.matmul(out=bias_ps[:], lhsT=ones[:], rhs=bias_row[:], start=True, stop=True)
-            nc.vector.tensor_copy(out=bias_all[:], in_=bias_ps[:])
+            nc.vector.tensor_scalar_mul(out=bias_all[:], in0=bias_ps[:], scalar1=1.0 / FEAT)
             norm_ps = psum.tile([P, P], F32, tag="tT_ps")
             nc.tensor.transpose(norm_ps[:], norm_rows_f32[:], ident[:])
-            nc.vector.tensor_copy(out=norm_cols[:], in_=norm_ps[:, 0 : 2 * HALVES])
+            nc.vector.tensor_scalar_mul(
+                out=gain_cols[:], in0=norm_ps[:, 0:HALVES], scalar1=float(FEAT)
+            )
+            nc.vector.tensor_copy(out=shift_cols[:], in_=norm_ps[:, HALVES : 2 * HALVES])
 
         kept = {}
 
@@ -128,10 +144,7 @@ def tile_dcadecoderblock_pb_t_kernel(
             grouped = work.tile([P, PAIR * P * PACK], BF16, align_bytes=64)
             side_by_side = grouped[:].bitcast(F32).rearrange("p (i r v) -> p i r v", i=PAIR, v=2)
             bank = kept["hT", u][:].rearrange("p (i v r) -> p i r v", i=PAIR, v=2)
-            if u % VECTOR_SHARE == VECTOR_SHARE - 1:
-                nc.vector.tensor_copy(out=side_by_side, in_=bank)
-            else:
-                nc.scalar.copy(out=side_by_side, in_=bank)
+            nc.scalar.copy(out=side_by_side, in_=bank)
             kept["grouped", u] = grouped
 
         def quantise_h(u):
@@ -159,41 +172,42 @@ def tile_dcadecoderblock_pb_t_kernel(
 
         def add_bias(u):
             o = long_lived.tile([P, PAIR, FEAT], F32)
-            row_sum = work.tile([P, PAIR], F32)
+            mean = long_lived.tile([P, PAIR], F32)
             for i in range(PAIR):
                 nc.vector.scalar_tensor_tensor(
                     out=o[:, i, :],
                     in0=kept["a", u][:, i, :],
-                    scalar=1.0,
+                    scalar=1.0 / FEAT,
                     in1=bias_all[:],
                     op0=ALU.mult,
                     op1=ALU.add,
-                    accum_out=row_sum[:, i : i + 1],
+                    accum_out=mean[:, i : i + 1],
                 )
             kept["o", u] = o
-            kept["row_sum", u] = row_sum
+            kept["mean", u] = mean
 
-        def negate_mean(u):
-            neg_mean = long_lived.tile([P, PAIR], F32)
+        def scale_mean(u):
+            mean_scaled = long_lived.tile([P, PAIR], F32)
             nc.gpsimd.tensor_scalar(
-                out=neg_mean[:],
-                in0=kept["row_sum", u][:],
+                out=mean_scaled[:],
+                in0=kept["mean", u][:],
                 scalar1=-1.0 / FEAT,
                 scalar2=0.0,
                 op0=ALU.mult,
                 op1=ALU.add,
             )
-            kept["neg_mean", u] = neg_mean
+            kept["mean_scaled", u] = mean_scaled
 
         def sum_squares(u):
-            squares = work.tile([P, PAIR, FEAT], F32)
             sum_sq = work.tile([P, PAIR], F32)
             for i in range(PAIR):
+                squares = work.tile([P, FEAT], F32)
                 nc.scalar.activation(
-                    out=squares[:, i, :],
+                    out=squares[:],
                     in_=kept["o", u][:, i, :],
                     func=ACT.Square,
-                    bias=kept["neg_mean", u][:, i : i + 1],
+                    scale=-float(FEAT),
+                    bias=kept["mean", u][:, i : i + 1],
                     accum_out=sum_sq[:, i : i + 1],
                 )
             kept["sum_sq", u] = sum_sq
@@ -212,10 +226,10 @@ def tile_dcadecoderblock_pb_t_kernel(
         def normalise(u):
             t = work.tile([P, PAIR, FEAT], F32)
             for i in range(PAIR):
-                nc.gpsimd.tensor_scalar(
+                nc.vector.tensor_scalar(
                     out=t[:, i, :],
                     in0=kept["o", u][:, i, :],
-                    scalar1=kept["neg_mean", u][:, i : i + 1],
+                    scalar1=kept["mean_scaled", u][:, i : i + 1],
                     scalar2=kept["rstd", u][:, i : i + 1],
                     op0=ALU.add,
                     op1=ALU.mult,
@@ -224,8 +238,8 @@ def tile_dcadecoderblock_pb_t_kernel(
 
         def features_to_partitions(u):
             tT_ps = psum.tile([P, HALVES, PAIR * P], F32)
-            for j in range(HALVES):
-                for i in range(PAIR):
+            for i in range(PAIR):
+                for j in range(HALVES):
                     nc.tensor.transpose(
                         tT_ps[:, j, i * P : (i + 1) * P],
                         kept["t", u][:, i, j * P : (j + 1) * P],
@@ -240,15 +254,15 @@ def tile_dcadecoderblock_pb_t_kernel(
                     out=yT[:, j, :],
                     in_=kept["tT", u][:, j, :],
                     func=ACT.Identity,
-                    scale=norm_cols[:, j : j + 1],
-                    bias=norm_cols[:, HALVES + j : HALVES + j + 1],
+                    scale=gain_cols[:, j : j + 1],
+                    bias=shift_cols[:, j : j + 1],
                 )
             kept["yT", u] = yT
 
         def rows_to_partitions(u):
             y_ps = psum.tile([P, PAIR, FEAT], F32)
-            for i in range(PAIR):
-                for j in range(HALVES):
+            for j in range(HALVES):
+                for i in range(PAIR):
                     nc.tensor.transpose(
                         y_ps[:, i, j * P : (j + 1) * P],
                         kept["yT", u][:, j, i * P : (i + 1) * P],
@@ -271,29 +285,25 @@ def tile_dcadecoderblock_pb_t_kernel(
             )
 
         stages = [
-            transpose_h,
-            regroup_h,
-            quantise_h,
-            project,
-            add_bias,
-            negate_mean,
-            sum_squares,
-            inverse_root,
-            normalise,
-            features_to_partitions,
-            gain_and_shift,
-            rows_to_partitions,
-            add_residual_and_store,
+            (transpose_h, 0),
+            (regroup_h, 1),
+            (quantise_h, 2),
+            (project, 3),
+            (add_bias, 4),
+            (scale_mean, 5),
+            (sum_squares, 5),
+            (inverse_root, 6),
+            (normalise, 7),
+            (features_to_partitions, 8),
+            (gain_and_shift, 9),
+            (rows_to_partitions, 10),
+            (add_residual_and_store, 11),
         ]
-
-        def one_round(s):
-            for n, stage in reversed(list(enumerate(stages))):
-                if 0 <= s - n < PAIRS:
-                    stage(s - n)
-
-        first_product = stages.index(project)
-        for s in range(first_product):
-            one_round(s)
-        spread_constants()
-        for s in range(first_product, PAIRS + len(stages) - 1):
-            one_round(s)
+        in_round = sorted(stages, key=lambda entry: -entry[1])
+        rounds = PAIRS + stages[-1][1]
+        for s in range(rounds):
+            if s == dict(stages)[project]:
+                spread_constants()
+            for stage, lag in in_round:
+                if 0 <= s - lag < PAIRS:
+                    stage(s - lag)

@@ -226,7 +226,7 @@ def tile_dcadecoderblock_pb_t_kernel(
         def normalise(u):
             t = work.tile([P, PAIR, FEAT], F32)
             for i in range(PAIR):
-                nc.vector.tensor_scalar(
+                nc.gpsimd.tensor_scalar(
                     out=t[:, i, :],
                     in0=kept["o", u][:, i, :],
                     scalar1=kept["mean_scaled", u][:, i : i + 1],

@@ -22,7 +22,9 @@ TILES = ROWS // P
 PAIR = 2
 PAIRS = TILES // PAIR
 CHUNK = 4
-X_LAG = 2
+X_CHUNK = 8
+FIRST_LOADS = ((1, 1, 2), (2, 2))
+DRAIN = 4
 EPS = 1e-5
 
 FLOPS = 2 * ROWS * K * FEAT
@@ -39,9 +41,10 @@ def tile_dcadecoderblock_pb_t_kernel(
     with ExitStack() as stack:
         consts = stack.enter_context(tc.tile_pool(name="consts", bufs=1))
         loads = stack.enter_context(tc.tile_pool(name="loads", bufs=TILES // CHUNK))
+        x_loads = stack.enter_context(tc.tile_pool(name="x_loads", bufs=TILES // X_CHUNK))
         work = stack.enter_context(tc.tile_pool(name="work", bufs=3))
         long_lived = stack.enter_context(tc.tile_pool(name="long_lived", bufs=6))
-        results = stack.enter_context(tc.tile_pool(name="results", bufs=10))
+        results = stack.enter_context(tc.tile_pool(name="results", bufs=32))
         psum = stack.enter_context(tc.psum_pool(name="psum", bufs=2))
         stack.enter_context(tc.manual_schedule())
 
@@ -73,49 +76,54 @@ def tile_dcadecoderblock_pb_t_kernel(
 
         def load_h(c, parts):
             h_sb = loads.tile([P, CHUNK * K], BF16)
-            step = CHUNK // parts
-            for j in range(parts):
+            first = 0
+            for step in parts:
                 nc.sync.dma_start(
-                    out=h_sb[:, j * step * K : (j + 1) * step * K].rearrange(
+                    out=h_sb[:, first * K : (first + step) * K].rearrange(
                         "p (i k) -> p i k", i=step
                     ),
-                    in_=h_rows[:, c * CHUNK + j * step : c * CHUNK + (j + 1) * step, :],
+                    in_=h_rows[:, c * CHUNK + first : c * CHUNK + first + step, :],
                 )
+                first += step
             h_chunks.append(h_sb)
 
         def load_x(c):
-            x_sb = loads.tile([P, CHUNK * FEAT], BF16)
+            x_sb = x_loads.tile([P, X_CHUNK * FEAT], BF16)
             nc.sync.dma_start(
-                out=x_sb[:].rearrange("p (i n) -> p i n", i=CHUNK),
-                in_=x_rows[:, c * CHUNK : (c + 1) * CHUNK, :],
+                out=x_sb[:].rearrange("p (i n) -> p i n", i=X_CHUNK),
+                in_=x_rows[:, c * X_CHUNK : (c + 1) * X_CHUNK, :],
             )
             x_chunks.append(x_sb)
 
-        for c in range(TILES // CHUNK + X_LAG):
-            if c < TILES // CHUNK:
-                load_h(c, 2 if c == 0 else 1)
-            if c >= X_LAG:
-                load_x(c - X_LAG)
+        for c in range(TILES // CHUNK):
+            load_h(c, FIRST_LOADS[c] if c < len(FIRST_LOADS) else (CHUNK,))
+            if c % 2 == 0 and c >= 2:
+                load_x(c // 2 - 1)
+        load_x(TILES // X_CHUNK - 1)
 
-        w_grouped = consts.tile([P, FEAT, PACK], BF16, align_bytes=64)
-        nc.vector.tensor_copy(out=w_grouped[:], in_=w_raw[:].rearrange("p t n -> p n t"))
         w_codes = consts.tile([P, FEAT], U32, align_bytes=64)
         w_scales = consts.tile([P, FEAT], U8, align_bytes=64)
-        nc.vector.quantize_mx(
-            out=w_codes[:].bitcast(FP8X4),
-            scales=w_scales[:],
-            in_=w_grouped[:].rearrange("p n t -> p (n t)"),
-        )
         norm_rows_f32 = consts.tile([P, P], F32)
-        nc.vector.tensor_copy(out=norm_rows_f32[:], in_=norm_rows[:])
         bias_all = consts.tile([P, FEAT], F32)
         gain_cols = consts.tile([P, HALVES], F32)
         shift_cols = consts.tile([P, HALVES], F32)
 
-        def spread_constants():
+        def quantise_w():
+            w_grouped = consts.tile([P, FEAT, PACK], BF16, align_bytes=64)
+            nc.vector.tensor_copy(out=w_grouped[:], in_=w_raw[:].rearrange("p t n -> p n t"))
+            nc.vector.quantize_mx(
+                out=w_codes[:].bitcast(FP8X4),
+                scales=w_scales[:],
+                in_=w_grouped[:].rearrange("p n t -> p (n t)"),
+            )
+
+        def spread_bias():
             bias_ps = psum.tile([P, FEAT], F32, tag="a_ps")
             nc.tensor.matmul(out=bias_ps[:], lhsT=ones[:], rhs=bias_row[:], start=True, stop=True)
             nc.vector.tensor_scalar_mul(out=bias_all[:], in0=bias_ps[:], scalar1=1.0 / FEAT)
+
+        def spread_gain_and_shift():
+            nc.vector.tensor_copy(out=norm_rows_f32[:], in_=norm_rows[:])
             norm_ps = psum.tile([P, P], F32, tag="tT_ps")
             nc.tensor.transpose(norm_ps[:], norm_rows_f32[:], ident[:])
             nc.vector.tensor_scalar_mul(
@@ -125,11 +133,16 @@ def tile_dcadecoderblock_pb_t_kernel(
 
         kept = {}
 
-        def transpose_h(u):
+        def tile_of(name, u, tiles, make):
+            if (name, u) not in kept:
+                kept[name, u] = make()
+            return kept[name, u]
+
+        def transpose_h(u, tiles):
             first = (u * PAIR % CHUNK) * WORDS
             h_words = h_chunks[u * PAIR // CHUNK][:].bitcast(F32)
-            hT_ps = psum.tile([P, PAIR * WORDS], F32)
-            for i in range(PAIR):
+            hT_ps = tile_of("hT", u, tiles, lambda: psum.tile([P, PAIR * WORDS], F32, name="hT_ps"))
+            for i in tiles:
                 row = first + i * WORDS
                 for v in range(2):
                     c = 2 * i + v
@@ -138,16 +151,27 @@ def tile_dcadecoderblock_pb_t_kernel(
                         h_words[:, row + v : row + WORDS : 2],
                         ident[:],
                     )
-            kept["hT", u] = hT_ps
 
-        def regroup_h(u):
-            grouped = work.tile([P, PAIR * P * PACK], BF16, align_bytes=64)
-            side_by_side = grouped[:].bitcast(F32).rearrange("p (i r v) -> p i r v", i=PAIR, v=2)
-            bank = kept["hT", u][:].rearrange("p (i v r) -> p i r v", i=PAIR, v=2)
-            nc.scalar.copy(out=side_by_side, in_=bank)
-            kept["grouped", u] = grouped
+        def regroup_h(u, tiles):
+            grouped = tile_of(
+                "grouped",
+                u,
+                tiles,
+                lambda: work.tile([P, PAIR * P * PACK], BF16, align_bytes=64, name="grouped"),
+            )
+            first, width = tiles[0] * WORDS, len(tiles) * WORDS
+            side_by_side = grouped[:].bitcast(F32)[:, first : first + width].rearrange(
+                "p (i r v) -> p i r v", r=P, v=2
+            )
+            bank = kept["hT", u][:, first : first + width].rearrange(
+                "p (i v r) -> p i r v", v=2, r=P
+            )
+            if u == 1 or u % 5 == 4:
+                nc.vector.tensor_copy(out=side_by_side, in_=bank)
+            else:
+                nc.scalar.copy(out=side_by_side, in_=bank)
 
-        def quantise_h(u):
+        def quantise_h(u, tiles):
             h_codes = work.tile([P, PAIR * P], U32, align_bytes=64)
             h_scales = work.tile([P, PAIR * P], U8, align_bytes=64)
             nc.vector.quantize_mx(
@@ -156,7 +180,7 @@ def tile_dcadecoderblock_pb_t_kernel(
             kept["codes", u] = h_codes
             kept["scales", u] = h_scales
 
-        def project(u):
+        def project(u, tiles):
             a_ps = psum.tile([P, PAIR, FEAT], F32)
             for i in range(PAIR):
                 nc.tensor.matmul_mx(
@@ -170,10 +194,10 @@ def tile_dcadecoderblock_pb_t_kernel(
                 )
             kept["a", u] = a_ps
 
-        def add_bias(u):
+        def add_bias(u, tiles):
             o = long_lived.tile([P, PAIR, FEAT], F32)
             mean = long_lived.tile([P, PAIR], F32)
-            for i in range(PAIR):
+            for i in reversed(range(PAIR)):
                 nc.vector.scalar_tensor_tensor(
                     out=o[:, i, :],
                     in0=kept["a", u][:, i, :],
@@ -186,7 +210,7 @@ def tile_dcadecoderblock_pb_t_kernel(
             kept["o", u] = o
             kept["mean", u] = mean
 
-        def scale_mean(u):
+        def scale_mean(u, tiles):
             mean_scaled = long_lived.tile([P, PAIR], F32)
             nc.gpsimd.tensor_scalar(
                 out=mean_scaled[:],
@@ -198,9 +222,9 @@ def tile_dcadecoderblock_pb_t_kernel(
             )
             kept["mean_scaled", u] = mean_scaled
 
-        def sum_squares(u):
-            sum_sq = work.tile([P, PAIR], F32)
-            for i in range(PAIR):
+        def sum_squares(u, tiles):
+            sum_sq = tile_of("sum_sq", u, tiles, lambda: work.tile([P, PAIR], F32, name="sum_sq"))
+            for i in reversed(tiles):
                 squares = work.tile([P, FEAT], F32)
                 nc.scalar.activation(
                     out=squares[:],
@@ -210,23 +234,23 @@ def tile_dcadecoderblock_pb_t_kernel(
                     bias=kept["mean", u][:, i : i + 1],
                     accum_out=sum_sq[:, i : i + 1],
                 )
-            kept["sum_sq", u] = sum_sq
 
-        def inverse_root(u):
-            rstd = work.tile([P, PAIR], F32)
+        def inverse_root(u, tiles):
+            rstd = tile_of("rstd", u, tiles, lambda: work.tile([P, PAIR], F32, name="rstd"))
+            columns = slice(tiles[0], tiles[0] + len(tiles))
             nc.scalar.activation(
-                out=rstd[:],
-                in_=kept["sum_sq", u][:],
+                out=rstd[:, columns],
+                in_=kept["sum_sq", u][:, columns],
                 func=ACT.Abs_reciprocal_sqrt,
                 scale=1.0 / FEAT,
                 bias=eps[:],
             )
-            kept["rstd", u] = rstd
 
-        def normalise(u):
-            t = work.tile([P, PAIR, FEAT], F32)
-            for i in range(PAIR):
-                nc.gpsimd.tensor_scalar(
+        def normalise(u, tiles):
+            t = tile_of("t", u, tiles, lambda: work.tile([P, PAIR, FEAT], F32, name="t"))
+            for i in tiles:
+                engine = nc.vector if u >= PAIRS - DRAIN else nc.gpsimd
+                engine.tensor_scalar(
                     out=t[:, i, :],
                     in0=kept["o", u][:, i, :],
                     scalar1=kept["mean_scaled", u][:, i : i + 1],
@@ -234,54 +258,56 @@ def tile_dcadecoderblock_pb_t_kernel(
                     op0=ALU.add,
                     op1=ALU.mult,
                 )
-            kept["t", u] = t
 
-        def features_to_partitions(u):
-            tT_ps = psum.tile([P, HALVES, PAIR * P], F32)
-            for i in range(PAIR):
+        def features_to_partitions(u, tiles):
+            tT_ps = tile_of(
+                "tT", u, tiles, lambda: psum.tile([P, HALVES, PAIR * P], F32, name="tT_ps")
+            )
+            for i in reversed(tiles):
                 for j in range(HALVES):
                     nc.tensor.transpose(
                         tT_ps[:, j, i * P : (i + 1) * P],
                         kept["t", u][:, i, j * P : (j + 1) * P],
                         ident[:],
                     )
-            kept["tT", u] = tT_ps
 
-        def gain_and_shift(u):
-            yT = work.tile([P, HALVES, PAIR * P], F32)
+        def gain_and_shift(u, tiles):
+            yT = tile_of("yT", u, tiles, lambda: work.tile([P, HALVES, PAIR * P], F32, name="yT"))
+            rows = slice(tiles[0] * P, (tiles[0] + len(tiles)) * P)
             for j in range(HALVES):
                 nc.scalar.activation(
-                    out=yT[:, j, :],
-                    in_=kept["tT", u][:, j, :],
+                    out=yT[:, j, rows],
+                    in_=kept["tT", u][:, j, rows],
                     func=ACT.Identity,
                     scale=gain_cols[:, j : j + 1],
                     bias=shift_cols[:, j : j + 1],
                 )
-            kept["yT", u] = yT
 
-        def rows_to_partitions(u):
-            y_ps = psum.tile([P, PAIR, FEAT], F32)
-            for j in range(HALVES):
-                for i in range(PAIR):
+        def rows_to_partitions(u, tiles):
+            y_ps = tile_of("y", u, tiles, lambda: psum.tile([P, PAIR, FEAT], F32, name="y_ps"))
+            for j in reversed(range(HALVES)):
+                for i in tiles:
                     nc.tensor.transpose(
                         y_ps[:, i, j * P : (j + 1) * P],
                         kept["yT", u][:, j, i * P : (i + 1) * P],
                         ident[:],
                     )
-            kept["y", u] = y_ps
 
-        def add_residual_and_store(u):
-            first = (u * PAIR % CHUNK) * FEAT
-            result = results.tile([P, PAIR * FEAT], F32)
+        def add_residual_and_store(u, tiles):
+            result = tile_of("result", u, tiles, lambda: results.tile([P, PAIR, FEAT], F32, name="result"))
+            first, width = tiles[0], len(tiles)
+            x_first = u * PAIR % X_CHUNK + first
             nc.vector.tensor_tensor(
-                out=result[:],
-                in0=kept["y", u][:].rearrange("p i n -> p (i n)"),
-                in1=x_chunks[u * PAIR // CHUNK][:, first : first + PAIR * FEAT],
+                out=result[:, first : first + width, :],
+                in0=kept["y", u][:, first : first + width, :],
+                in1=x_chunks[u * PAIR // X_CHUNK][:].rearrange("p (i n) -> p i n", i=X_CHUNK)[
+                    :, x_first : x_first + width, :
+                ],
                 op=ALU.add,
             )
+            row = u * PAIR + first
             nc.sync.dma_start(
-                out=out_rows[:, u * PAIR : (u + 1) * PAIR, :],
-                in_=result[:].rearrange("p (i n) -> p i n", i=PAIR),
+                out=out_rows[:, row : row + width, :], in_=result[:, first : first + width, :]
             )
 
         stages = [
@@ -300,10 +326,30 @@ def tile_dcadecoderblock_pb_t_kernel(
             (add_residual_and_store, 11),
         ]
         in_round = sorted(stages, key=lambda entry: -entry[1])
+        by_tile_first = [transpose_h, regroup_h]
+        by_tile_last = [
+            sum_squares,
+            inverse_root,
+            normalise,
+            features_to_partitions,
+            gain_and_shift,
+            rows_to_partitions,
+            add_residual_and_store,
+        ]
         rounds = PAIRS + stages[-1][1]
         for s in range(rounds):
+            if s == dict(stages)[regroup_h] + 1:
+                quantise_w()
             if s == dict(stages)[project]:
-                spread_constants()
+                spread_bias()
+            if s == dict(stages)[inverse_root]:
+                spread_gain_and_shift()
             for stage, lag in in_round:
-                if 0 <= s - lag < PAIRS:
-                    stage(s - lag)
+                u = s - lag
+                if not 0 <= u < PAIRS:
+                    continue
+                if (stage in by_tile_first and u < 1) or (stage in by_tile_last and u >= PAIRS - 1):
+                    stage(u, (0,))
+                    stage(u, (1,))
+                else:
+                    stage(u, (0, 1))

@@ -25,6 +25,7 @@ CHUNK = 4
 X_CHUNK = 8
 FIRST_LOADS = ((1, 1, 2), (2, 2))
 DRAIN = 4
+ROW_GAIN_EVERY = 8
 EPS = 1e-5
 
 FLOPS = 2 * ROWS * K * FEAT
@@ -43,8 +44,9 @@ def tile_dcadecoderblock_pb_t_kernel(
         loads = stack.enter_context(tc.tile_pool(name="loads", bufs=TILES // CHUNK))
         x_loads = stack.enter_context(tc.tile_pool(name="x_loads", bufs=TILES // X_CHUNK))
         work = stack.enter_context(tc.tile_pool(name="work", bufs=3))
-        long_lived = stack.enter_context(tc.tile_pool(name="long_lived", bufs=6))
+        long_lived = stack.enter_context(tc.tile_pool(name="long_lived", bufs=8))
         results = stack.enter_context(tc.tile_pool(name="results", bufs=32))
+        late = stack.enter_context(tc.tile_pool(name="late", bufs=4))
         psum = stack.enter_context(tc.psum_pool(name="psum", bufs=2))
         stack.enter_context(tc.manual_schedule())
 
@@ -53,6 +55,10 @@ def tile_dcadecoderblock_pb_t_kernel(
 
         w_raw = consts.tile([P, PACK, FEAT], BF16)
         nc.scalar.dma_start(out=w_raw[:], in_=attn_out_W.rearrange("(p t) n -> p t n", t=PACK))
+        eps = consts.tile([P, 1], F32)
+        nc.vector.memset(eps[:], EPS)
+        table_warm = consts.tile([P, 1], F32)
+        nc.scalar.activation(out=table_warm[:], in_=eps[:], func=ACT.Abs_reciprocal_sqrt)
         bias_row = consts.tile([P, FEAT], BF16)
         nc.vector.memset(bias_row[:], 0.0)
         nc.scalar.dma_start(out=bias_row[0:1, :], in_=attn_out_b.rearrange("(o n) -> o n", o=1))
@@ -66,10 +72,8 @@ def tile_dcadecoderblock_pb_t_kernel(
         )
         ones = consts.tile([P, P], BF16)
         nc.vector.memset(ones[:], 1.0)
-        eps = consts.tile([P, 1], F32)
-        nc.vector.memset(eps[:], EPS)
-        table_warm = consts.tile([P, 1], F32)
-        nc.scalar.activation(out=table_warm[:], in_=eps[:], func=ACT.Abs_reciprocal_sqrt)
+        rows = consts.tile([P, 1 + PAIR, FEAT], BF16)
+        nc.vector.memset(rows[:], 0.0)
 
         h_chunks = []
         x_chunks = []
@@ -99,12 +103,20 @@ def tile_dcadecoderblock_pb_t_kernel(
             load_h(c, FIRST_LOADS[c] if c < len(FIRST_LOADS) else (CHUNK,))
             if c % 2 == 0 and c >= 2:
                 load_x(c // 2 - 1)
+            if c == 1:
+                nc.sync.dma_start(out=rows[0:1, 0, :], in_=attn_norm_g.rearrange("(o n) -> o n", o=1))
+                for i in range(PAIR):
+                    nc.sync.dma_start(
+                        out=rows[0:1, 1 + i, :], in_=attn_norm_b.rearrange("(o n) -> o n", o=1)
+                    )
         load_x(TILES // X_CHUNK - 1)
 
         w_codes = consts.tile([P, FEAT], U32, align_bytes=64)
         w_scales = consts.tile([P, FEAT], U8, align_bytes=64)
         norm_rows_f32 = consts.tile([P, P], F32)
         bias_all = consts.tile([P, FEAT], F32)
+        gain_all = consts.tile([P, FEAT], F32)
+        ident_bf16 = consts.tile([P, P], BF16)
         gain_cols = consts.tile([P, HALVES], F32)
         shift_cols = consts.tile([P, HALVES], F32)
 
@@ -130,6 +142,15 @@ def tile_dcadecoderblock_pb_t_kernel(
                 out=gain_cols[:], in0=norm_ps[:, 0:HALVES], scalar1=float(FEAT)
             )
             nc.vector.tensor_copy(out=shift_cols[:], in_=norm_ps[:, HALVES : 2 * HALVES])
+            gain_ps = psum.tile([P, FEAT], F32, tag="tT_ps")
+            nc.tensor.matmul(out=gain_ps[:], lhsT=ones[:], rhs=rows[:, 0, :], start=True, stop=True)
+            nc.vector.tensor_scalar_mul(out=gain_all[:], in0=gain_ps[:], scalar1=float(FEAT))
+            nc.vector.tensor_copy(out=ident_bf16[:], in_=ident[:])
+
+        def kind(u):
+            if u == PAIRS - 1:
+                return "late"
+            return "vector" if u % ROW_GAIN_EVERY == ROW_GAIN_EVERY // 2 else "tensor"
 
         kept = {}
 
@@ -166,7 +187,7 @@ def tile_dcadecoderblock_pb_t_kernel(
             bank = kept["hT", u][:, first : first + width].rearrange(
                 "p (i v r) -> p i r v", v=2, r=P
             )
-            if u == 1 or u % 5 == 4:
+            if u == 1 or u % 16 == 7:
                 nc.vector.tensor_copy(out=side_by_side, in_=bank)
             else:
                 nc.scalar.copy(out=side_by_side, in_=bank)
@@ -236,7 +257,7 @@ def tile_dcadecoderblock_pb_t_kernel(
                 )
 
         def inverse_root(u, tiles):
-            rstd = tile_of("rstd", u, tiles, lambda: work.tile([P, PAIR], F32, name="rstd"))
+            rstd = tile_of("rstd", u, tiles, lambda: long_lived.tile([P, PAIR], F32, name="rstd"))
             columns = slice(tiles[0], tiles[0] + len(tiles))
             nc.scalar.activation(
                 out=rstd[:, columns],
@@ -255,6 +276,36 @@ def tile_dcadecoderblock_pb_t_kernel(
                     in0=kept["o", u][:, i, :],
                     scalar1=kept["mean_scaled", u][:, i : i + 1],
                     scalar2=kept["rstd", u][:, i : i + 1],
+                    op0=ALU.add,
+                    op1=ALU.mult,
+                )
+
+        def x_rows_of(u, tiles):
+            x_first = u * PAIR % X_CHUNK + tiles[0]
+            x_sb = x_chunks[u * PAIR // X_CHUNK][:].rearrange("p (i n) -> p i n", i=X_CHUNK)
+            return x_sb[:, x_first : x_first + len(tiles), :]
+
+        def add_shift_to_x(u, tiles):
+            tag = "hT_ps" if kind(u) == "late" else "y_ps"
+            x_ps = psum.tile([P, PAIR, FEAT], F32, tag=tag)
+            nc.tensor.matmul(
+                out=x_ps[:], lhsT=ident_bf16[:], rhs=x_rows_of(u, tiles), start=True, stop=False
+            )
+            nc.tensor.matmul(
+                out=x_ps[:], lhsT=ones[:], rhs=rows[:, 1 : 1 + PAIR, :], start=False, stop=True
+            )
+            kept["x_ps", u] = x_ps
+
+        def gain_on_vector(u, tiles):
+            scaled = tile_of(
+                "scaled", u, tiles, lambda: late.tile([P, PAIR, FEAT], F32, name="scaled")
+            )
+            for i in reversed(tiles):
+                nc.vector.scalar_tensor_tensor(
+                    out=scaled[:, i, :],
+                    in0=kept["o", u][:, i, :],
+                    scalar=kept["mean_scaled", u][:, i : i + 1],
+                    in1=gain_all[:],
                     op0=ALU.add,
                     op1=ALU.mult,
                 )
@@ -296,60 +347,97 @@ def tile_dcadecoderblock_pb_t_kernel(
         def add_residual_and_store(u, tiles):
             result = tile_of("result", u, tiles, lambda: results.tile([P, PAIR, FEAT], F32, name="result"))
             first, width = tiles[0], len(tiles)
-            x_first = u * PAIR % X_CHUNK + first
-            nc.vector.tensor_tensor(
-                out=result[:, first : first + width, :],
-                in0=kept["y", u][:, first : first + width, :],
-                in1=x_chunks[u * PAIR // X_CHUNK][:].rearrange("p (i n) -> p i n", i=X_CHUNK)[
-                    :, x_first : x_first + width, :
-                ],
-                op=ALU.add,
-            )
+            columns = slice(first, first + width)
+            if kind(u) != "tensor":
+                for i in tiles:
+                    nc.vector.scalar_tensor_tensor(
+                        out=result[:, i, :],
+                        in0=kept["scaled", u][:, i, :],
+                        scalar=kept["rstd", u][:, i : i + 1],
+                        in1=kept["x_ps", u][:, i, :],
+                        op0=ALU.mult,
+                        op1=ALU.add,
+                    )
+            else:
+                nc.vector.tensor_tensor(
+                    out=result[:, columns, :],
+                    in0=kept["y", u][:, columns, :],
+                    in1=x_rows_of(u, tiles),
+                    op=ALU.add,
+                )
             row = u * PAIR + first
             nc.sync.dma_start(
                 out=out_rows[:, row : row + width, :], in_=result[:, first : first + width, :]
             )
 
-        stages = [
-            (transpose_h, 0),
-            (regroup_h, 1),
-            (quantise_h, 2),
-            (project, 3),
-            (add_bias, 4),
-            (scale_mean, 5),
-            (sum_squares, 5),
-            (inverse_root, 6),
-            (normalise, 7),
-            (features_to_partitions, 8),
-            (gain_and_shift, 9),
-            (rows_to_partitions, 10),
-            (add_residual_and_store, 11),
+        both = (0, 1)
+        front = [
+            (sum_squares, 5, both),
+            (add_bias, 4, both),
+            (project, 3, both),
+            (quantise_h, 2, both),
+            (regroup_h, 1, both),
+            (transpose_h, 0, both),
         ]
-        in_round = sorted(stages, key=lambda entry: -entry[1])
-        by_tile_first = [transpose_h, regroup_h]
-        by_tile_last = [
-            sum_squares,
-            inverse_root,
-            normalise,
-            features_to_partitions,
-            gain_and_shift,
-            rows_to_partitions,
+        stages = {
+            "tensor": [
+                (add_residual_and_store, 11, both),
+                (rows_to_partitions, 10, both),
+                (gain_and_shift, 9, both),
+                (features_to_partitions, 8, both),
+                (normalise, 7, both),
+                (inverse_root, 6, both),
+                (scale_mean, 5, both),
+            ]
+            + front,
+            "vector": [
+                (add_residual_and_store, 11, both),
+                (gain_on_vector, 10, both),
+                (add_shift_to_x, 10, both),
+                (inverse_root, 6, both),
+                (scale_mean, 5, both),
+            ]
+            + front,
+            "late": [
+                (add_residual_and_store, 8, both),
+                (gain_on_vector, 7, both),
+                (add_shift_to_x, 5, both),
+                (inverse_root, 6, both),
+                (scale_mean, 5, both),
+            ]
+            + front,
+        }
+        order = [
             add_residual_and_store,
+            rows_to_partitions,
+            add_shift_to_x,
+            gain_and_shift,
+            features_to_partitions,
+            gain_on_vector,
+            normalise,
+            inverse_root,
+            scale_mean,
+            sum_squares,
+            add_bias,
+            project,
+            quantise_h,
+            regroup_h,
+            transpose_h,
         ]
-        rounds = PAIRS + stages[-1][1]
-        for s in range(rounds):
-            if s == dict(stages)[regroup_h] + 1:
+        last_lag = stages["tensor"][0][1]
+        for s in range(PAIRS + last_lag):
+            if s == 2:
                 quantise_w()
-            if s == dict(stages)[project]:
+            if s == 3:
                 spread_bias()
-            if s == dict(stages)[inverse_root]:
+            if s == 6:
                 spread_gain_and_shift()
-            for stage, lag in in_round:
-                u = s - lag
-                if not 0 <= u < PAIRS:
-                    continue
-                if (stage in by_tile_first and u < 1) or (stage in by_tile_last and u >= PAIRS - 1):
-                    stage(u, (0,))
-                    stage(u, (1,))
-                else:
-                    stage(u, (0, 1))
+            calls = []
+            for u in range(max(0, s - last_lag), min(s + 1, PAIRS)):
+                calls.extend((order.index(st), u, st, t) for st, lag, t in stages[kind(u)] if u + lag == s)
+            for place, u, stage, tiles in sorted(calls, key=lambda call: call[:2]):
+                by_tile = (u < 1 and stage in (transpose_h, regroup_h)) or (
+                    u == PAIRS - 1 and stage in (sum_squares, inverse_root, add_residual_and_store)
+                )
+                for part in [(i,) for i in tiles] if by_tile else [tiles]:
+                    stage(u, part)

from contextlib import ExitStack

import concourse.mybir as mybir
from concourse.masks import make_identity

F32 = mybir.dt.float32
BF16 = mybir.dt.bfloat16
U32 = mybir.dt.uint32
U8 = mybir.dt.uint8
FP8X4 = mybir.dt.float8_e4m3fn_x4
ALU = mybir.AluOpType
ACT = mybir.ActivationFunctionType

P = 128
PACK = 4
ROWS = 4 * 2048
K = 512
FEAT = 256
HALVES = FEAT // P
WORDS = K // 2
TILES = ROWS // P
PAIR = 2
PAIRS = TILES // PAIR
CHUNK = 4
X_CHUNK = 8
FIRST_LOADS = ((1, 1, 2), (2, 2))
DRAIN = 4
ROW_GAIN_EVERY = 8
EPS = 1e-5

FLOPS = 2 * ROWS * K * FEAT


def tile_dcadecoderblock_pb_t_kernel(
    tc, h_attn, x, attn_out_W, attn_out_b, attn_norm_g, attn_norm_b, out
):
    nc = tc.nc
    h_rows = h_attn.flatten_outer_dims().rearrange("(p j) k -> p j k", j=TILES)
    x_rows = x.flatten_outer_dims().rearrange("(p j) n -> p j n", j=TILES)
    out_rows = out.flatten_outer_dims().rearrange("(p j) n -> p j n", j=TILES)

    with ExitStack() as stack:
        consts = stack.enter_context(tc.tile_pool(name="consts", bufs=1))
        loads = stack.enter_context(tc.tile_pool(name="loads", bufs=TILES // CHUNK))
        x_loads = stack.enter_context(tc.tile_pool(name="x_loads", bufs=TILES // X_CHUNK))
        work = stack.enter_context(tc.tile_pool(name="work", bufs=3))
        long_lived = stack.enter_context(tc.tile_pool(name="long_lived", bufs=8))
        results = stack.enter_context(tc.tile_pool(name="results", bufs=32))
        late = stack.enter_context(tc.tile_pool(name="late", bufs=4))
        psum = stack.enter_context(tc.psum_pool(name="psum", bufs=2))
        stack.enter_context(tc.manual_schedule())

        ident = consts.tile([P, P], F32)
        make_identity(nc, ident[:])

        w_raw = consts.tile([P, PACK, FEAT], BF16)
        nc.scalar.dma_start(out=w_raw[:], in_=attn_out_W.rearrange("(p t) n -> p t n", t=PACK))
        eps = consts.tile([P, 1], F32)
        nc.vector.memset(eps[:], EPS)
        table_warm = consts.tile([P, 1], F32)
        nc.scalar.activation(out=table_warm[:], in_=eps[:], func=ACT.Abs_reciprocal_sqrt)
        bias_row = consts.tile([P, FEAT], BF16)
        nc.vector.memset(bias_row[:], 0.0)
        nc.scalar.dma_start(out=bias_row[0:1, :], in_=attn_out_b.rearrange("(o n) -> o n", o=1))
        norm_rows = consts.tile([P, P], BF16)
        nc.vector.memset(norm_rows[:], 0.0)
        nc.scalar.dma_start(
            out=norm_rows[0:HALVES, :], in_=attn_norm_g.rearrange("(j p) -> j p", p=P)
        )
        nc.scalar.dma_start(
            out=norm_rows[HALVES : 2 * HALVES, :], in_=attn_norm_b.rearrange("(j p) -> j p", p=P)
        )
        ones = consts.tile([P, P], BF16)
        nc.vector.memset(ones[:], 1.0)
        rows = consts.tile([P, 1 + PAIR, FEAT], BF16)
        nc.vector.memset(rows[:], 0.0)

        h_chunks = []
        x_chunks = []

        def load_h(c, parts):
            h_sb = loads.tile([P, CHUNK * K], BF16)
            first = 0
            for step in parts:
                nc.sync.dma_start(
                    out=h_sb[:, first * K : (first + step) * K].rearrange(
                        "p (i k) -> p i k", i=step
                    ),
                    in_=h_rows[:, c * CHUNK + first : c * CHUNK + first + step, :],
                )
                first += step
            h_chunks.append(h_sb)

        def load_x(c):
            x_sb = x_loads.tile([P, X_CHUNK * FEAT], BF16)
            nc.sync.dma_start(
                out=x_sb[:].rearrange("p (i n) -> p i n", i=X_CHUNK),
                in_=x_rows[:, c * X_CHUNK : (c + 1) * X_CHUNK, :],
            )
            x_chunks.append(x_sb)

        for c in range(TILES // CHUNK):
            load_h(c, FIRST_LOADS[c] if c < len(FIRST_LOADS) else (CHUNK,))
            if c % 2 == 0 and c >= 2:
                load_x(c // 2 - 1)
            if c == 1:
                nc.sync.dma_start(out=rows[0:1, 0, :], in_=attn_norm_g.rearrange("(o n) -> o n", o=1))
                for i in range(PAIR):
                    nc.sync.dma_start(
                        out=rows[0:1, 1 + i, :], in_=attn_norm_b.rearrange("(o n) -> o n", o=1)
                    )
        load_x(TILES // X_CHUNK - 1)

        w_codes = consts.tile([P, FEAT], U32, align_bytes=64)
        w_scales = consts.tile([P, FEAT], U8, align_bytes=64)
        norm_rows_f32 = consts.tile([P, P], F32)
        bias_all = consts.tile([P, FEAT], F32)
        gain_all = consts.tile([P, FEAT], F32)
        ident_bf16 = consts.tile([P, P], BF16)
        gain_cols = consts.tile([P, HALVES], F32)
        shift_cols = consts.tile([P, HALVES], F32)

        def quantise_w():
            w_grouped = consts.tile([P, FEAT, PACK], BF16, align_bytes=64)
            nc.vector.tensor_copy(out=w_grouped[:], in_=w_raw[:].rearrange("p t n -> p n t"))
            nc.vector.quantize_mx(
                out=w_codes[:].bitcast(FP8X4),
                scales=w_scales[:],
                in_=w_grouped[:].rearrange("p n t -> p (n t)"),
            )

        def spread_bias():
            bias_ps = psum.tile([P, FEAT], F32, tag="a_ps")
            nc.tensor.matmul(out=bias_ps[:], lhsT=ones[:], rhs=bias_row[:], start=True, stop=True)
            nc.vector.tensor_scalar_mul(out=bias_all[:], in0=bias_ps[:], scalar1=1.0 / FEAT)

        def spread_gain_and_shift():
            nc.vector.tensor_copy(out=norm_rows_f32[:], in_=norm_rows[:])
            norm_ps = psum.tile([P, P], F32, tag="tT_ps")
            nc.tensor.transpose(norm_ps[:], norm_rows_f32[:], ident[:])
            nc.vector.tensor_scalar_mul(
                out=gain_cols[:], in0=norm_ps[:, 0:HALVES], scalar1=float(FEAT)
            )
            nc.vector.tensor_copy(out=shift_cols[:], in_=norm_ps[:, HALVES : 2 * HALVES])
            gain_ps = psum.tile([P, FEAT], F32, tag="tT_ps")
            nc.tensor.matmul(out=gain_ps[:], lhsT=ones[:], rhs=rows[:, 0, :], start=True, stop=True)
            nc.vector.tensor_scalar_mul(out=gain_all[:], in0=gain_ps[:], scalar1=float(FEAT))
            nc.vector.tensor_copy(out=ident_bf16[:], in_=ident[:])

        def kind(u):
            if u == PAIRS - 1:
                return "late"
            return "vector" if u % ROW_GAIN_EVERY == ROW_GAIN_EVERY // 2 else "tensor"

        kept = {}

        def tile_of(name, u, tiles, make):
            if (name, u) not in kept:
                kept[name, u] = make()
            return kept[name, u]

        def transpose_h(u, tiles):
            first = (u * PAIR % CHUNK) * WORDS
            h_words = h_chunks[u * PAIR // CHUNK][:].bitcast(F32)
            hT_ps = tile_of("hT", u, tiles, lambda: psum.tile([P, PAIR * WORDS], F32, name="hT_ps"))
            for i in tiles:
                row = first + i * WORDS
                for v in range(2):
                    c = 2 * i + v
                    nc.tensor.transpose(
                        hT_ps[:, c * P : (c + 1) * P],
                        h_words[:, row + v : row + WORDS : 2],
                        ident[:],
                    )

        def regroup_h(u, tiles):
            grouped = tile_of(
                "grouped",
                u,
                tiles,
                lambda: work.tile([P, PAIR * P * PACK], BF16, align_bytes=64, name="grouped"),
            )
            first, width = tiles[0] * WORDS, len(tiles) * WORDS
            side_by_side = grouped[:].bitcast(F32)[:, first : first + width].rearrange(
                "p (i r v) -> p i r v", r=P, v=2
            )
            bank = kept["hT", u][:, first : first + width].rearrange(
                "p (i v r) -> p i r v", v=2, r=P
            )
            if u == 1 or u % 16 == 7:
                nc.vector.tensor_copy(out=side_by_side, in_=bank)
            else:
                nc.scalar.copy(out=side_by_side, in_=bank)

        def quantise_h(u, tiles):
            h_codes = work.tile([P, PAIR * P], U32, align_bytes=64)
            h_scales = work.tile([P, PAIR * P], U8, align_bytes=64)
            nc.vector.quantize_mx(
                out=h_codes[:].bitcast(FP8X4), scales=h_scales[:], in_=kept["grouped", u][:]
            )
            kept["codes", u] = h_codes
            kept["scales", u] = h_scales

        def project(u, tiles):
            a_ps = psum.tile([P, PAIR, FEAT], F32)
            for i in range(PAIR):
                nc.tensor.matmul_mx(
                    out=a_ps[:, i, :],
                    lhsT=kept["codes", u][:, i * P : (i + 1) * P].bitcast(FP8X4),
                    lhsT_scale=kept["scales", u][:, i * P : (i + 1) * P],
                    rhs=w_codes[:].bitcast(FP8X4),
                    rhs_scale=w_scales[:],
                    start=True,
                    stop=True,
                )
            kept["a", u] = a_ps

        def add_bias(u, tiles):
            o = long_lived.tile([P, PAIR, FEAT], F32)
            mean = long_lived.tile([P, PAIR], F32)
            for i in reversed(range(PAIR)):
                nc.vector.scalar_tensor_tensor(
                    out=o[:, i, :],
                    in0=kept["a", u][:, i, :],
                    scalar=1.0 / FEAT,
                    in1=bias_all[:],
                    op0=ALU.mult,
                    op1=ALU.add,
                    accum_out=mean[:, i : i + 1],
                )
            kept["o", u] = o
            kept["mean", u] = mean

        def scale_mean(u, tiles):
            mean_scaled = long_lived.tile([P, PAIR], F32)
            nc.gpsimd.tensor_scalar(
                out=mean_scaled[:],
                in0=kept["mean", u][:],
                scalar1=-1.0 / FEAT,
                scalar2=0.0,
                op0=ALU.mult,
                op1=ALU.add,
            )
            kept["mean_scaled", u] = mean_scaled

        def sum_squares(u, tiles):
            sum_sq = tile_of("sum_sq", u, tiles, lambda: work.tile([P, PAIR], F32, name="sum_sq"))
            for i in reversed(tiles):
                squares = work.tile([P, FEAT], F32)
                nc.scalar.activation(
                    out=squares[:],
                    in_=kept["o", u][:, i, :],
                    func=ACT.Square,
                    scale=-float(FEAT),
                    bias=kept["mean", u][:, i : i + 1],
                    accum_out=sum_sq[:, i : i + 1],
                )

        def inverse_root(u, tiles):
            rstd = tile_of("rstd", u, tiles, lambda: long_lived.tile([P, PAIR], F32, name="rstd"))
            columns = slice(tiles[0], tiles[0] + len(tiles))
            nc.scalar.activation(
                out=rstd[:, columns],
                in_=kept["sum_sq", u][:, columns],
                func=ACT.Abs_reciprocal_sqrt,
                scale=1.0 / FEAT,
                bias=eps[:],
            )

        def normalise(u, tiles):
            t = tile_of("t", u, tiles, lambda: work.tile([P, PAIR, FEAT], F32, name="t"))
            for i in tiles:
                engine = nc.vector if u >= PAIRS - DRAIN else nc.gpsimd
                engine.tensor_scalar(
                    out=t[:, i, :],
                    in0=kept["o", u][:, i, :],
                    scalar1=kept["mean_scaled", u][:, i : i + 1],
                    scalar2=kept["rstd", u][:, i : i + 1],
                    op0=ALU.add,
                    op1=ALU.mult,
                )

        def x_rows_of(u, tiles):
            x_first = u * PAIR % X_CHUNK + tiles[0]
            x_sb = x_chunks[u * PAIR // X_CHUNK][:].rearrange("p (i n) -> p i n", i=X_CHUNK)
            return x_sb[:, x_first : x_first + len(tiles), :]

        def add_shift_to_x(u, tiles):
            tag = "hT_ps" if kind(u) == "late" else "y_ps"
            x_ps = psum.tile([P, PAIR, FEAT], F32, tag=tag)
            nc.tensor.matmul(
                out=x_ps[:], lhsT=ident_bf16[:], rhs=x_rows_of(u, tiles), start=True, stop=False
            )
            nc.tensor.matmul(
                out=x_ps[:], lhsT=ones[:], rhs=rows[:, 1 : 1 + PAIR, :], start=False, stop=True
            )
            kept["x_ps", u] = x_ps

        def gain_on_vector(u, tiles):
            scaled = tile_of(
                "scaled", u, tiles, lambda: late.tile([P, PAIR, FEAT], F32, name="scaled")
            )
            for i in reversed(tiles):
                nc.vector.scalar_tensor_tensor(
                    out=scaled[:, i, :],
                    in0=kept["o", u][:, i, :],
                    scalar=kept["mean_scaled", u][:, i : i + 1],
                    in1=gain_all[:],
                    op0=ALU.add,
                    op1=ALU.mult,
                )

        def features_to_partitions(u, tiles):
            tT_ps = tile_of(
                "tT", u, tiles, lambda: psum.tile([P, HALVES, PAIR * P], F32, name="tT_ps")
            )
            for i in reversed(tiles):
                for j in range(HALVES):
                    nc.tensor.transpose(
                        tT_ps[:, j, i * P : (i + 1) * P],
                        kept["t", u][:, i, j * P : (j + 1) * P],
                        ident[:],
                    )

        def gain_and_shift(u, tiles):
            yT = tile_of("yT", u, tiles, lambda: work.tile([P, HALVES, PAIR * P], F32, name="yT"))
            rows = slice(tiles[0] * P, (tiles[0] + len(tiles)) * P)
            for j in range(HALVES):
                nc.scalar.activation(
                    out=yT[:, j, rows],
                    in_=kept["tT", u][:, j, rows],
                    func=ACT.Identity,
                    scale=gain_cols[:, j : j + 1],
                    bias=shift_cols[:, j : j + 1],
                )

        def rows_to_partitions(u, tiles):
            y_ps = tile_of("y", u, tiles, lambda: psum.tile([P, PAIR, FEAT], F32, name="y_ps"))
            for j in reversed(range(HALVES)):
                for i in tiles:
                    nc.tensor.transpose(
                        y_ps[:, i, j * P : (j + 1) * P],
                        kept["yT", u][:, j, i * P : (i + 1) * P],
                        ident[:],
                    )

        def add_residual_and_store(u, tiles):
            result = tile_of("result", u, tiles, lambda: results.tile([P, PAIR, FEAT], F32, name="result"))
            first, width = tiles[0], len(tiles)
            columns = slice(first, first + width)
            if kind(u) != "tensor":
                for i in tiles:
                    nc.vector.scalar_tensor_tensor(
                        out=result[:, i, :],
                        in0=kept["scaled", u][:, i, :],
                        scalar=kept["rstd", u][:, i : i + 1],
                        in1=kept["x_ps", u][:, i, :],
                        op0=ALU.mult,
                        op1=ALU.add,
                    )
            else:
                nc.vector.tensor_tensor(
                    out=result[:, columns, :],
                    in0=kept["y", u][:, columns, :],
                    in1=x_rows_of(u, tiles),
                    op=ALU.add,
                )
            row = u * PAIR + first
            nc.sync.dma_start(
                out=out_rows[:, row : row + width, :], in_=result[:, first : first + width, :]
            )

        both = (0, 1)
        front = [
            (sum_squares, 5, both),
            (add_bias, 4, both),
            (project, 3, both),
            (quantise_h, 2, both),
            (regroup_h, 1, both),
            (transpose_h, 0, both),
        ]
        stages = {
            "tensor": [
                (add_residual_and_store, 11, both),
                (rows_to_partitions, 10, both),
                (gain_and_shift, 9, both),
                (features_to_partitions, 8, both),
                (normalise, 7, both),
                (inverse_root, 6, both),
                (scale_mean, 5, both),
            ]
            + front,
            "vector": [
                (add_residual_and_store, 11, both),
                (gain_on_vector, 10, both),
                (add_shift_to_x, 10, both),
                (inverse_root, 6, both),
                (scale_mean, 5, both),
            ]
            + front,
            "late": [
                (add_residual_and_store, 8, both),
                (gain_on_vector, 7, both),
                (add_shift_to_x, 5, both),
                (inverse_root, 6, both),
                (scale_mean, 5, both),
            ]
            + front,
        }
        order = [
            add_residual_and_store,
            rows_to_partitions,
            add_shift_to_x,
            gain_and_shift,
            features_to_partitions,
            gain_on_vector,
            normalise,
            inverse_root,
            scale_mean,
            sum_squares,
            add_bias,
            project,
            quantise_h,
            regroup_h,
            transpose_h,
        ]
        last_lag = stages["tensor"][0][1]
        for s in range(PAIRS + last_lag):
            if s == 2:
                quantise_w()
            if s == 3:
                spread_bias()
            if s == 6:
                spread_gain_and_shift()
            calls = []
            for u in range(max(0, s - last_lag), min(s + 1, PAIRS)):
                calls.extend((order.index(st), u, st, t) for st, lag, t in stages[kind(u)] if u + lag == s)
            for place, u, stage, tiles in sorted(calls, key=lambda call: call[:2]):
                by_tile = (u < 1 and stage in (transpose_h, regroup_h)) or (
                    u == PAIRS - 1 and stage in (sum_squares, inverse_root, add_residual_and_store)
                )
                for part in [(i,) for i in tiles] if by_tile else [tiles]:
                    stage(u, part)
